import numpy as np
import ml_dtypes


def mxq(x, axis, fmt="e4m3"):
    dtype, down = {"e4m3": (ml_dtypes.float8_e4m3fn, 7), "e5m2": (ml_dtypes.float8_e5m2, 14)}[fmt]
    v = np.moveaxis(np.asarray(x, np.float32).astype(ml_dtypes.bfloat16).astype(np.float64), axis, -1)
    blocks = v.reshape(v.shape[:-1] + (-1, 32))
    amax = np.abs(blocks).max(-1, keepdims=True)
    byte = np.maximum(np.where(amax > 0, np.frexp(amax)[1] - 1 + 127, 0) - down, 1)
    scale = np.exp2(byte - 127.0)
    codes = (blocks / scale).astype(np.float32).astype(dtype).astype(np.float64)
    return np.moveaxis((codes * scale).reshape(v.shape), -1, axis)


WIDE = False


def mx_kscale(k):
    if not WIDE:
        return np.ones(k)
    levels = np.array([10, -10, 5, -5, 0])
    a = np.random.permutation(np.resize(levels, k // 512 * 4)).reshape(k // 512, 4)
    idx = np.arange(k)
    return np.exp2(a[idx // 512, idx % 128 // 32])


BF16 = ml_dtypes.bfloat16


def bf(x):
    return np.asarray(x, np.float32).astype(BF16)


def f64(x):
    return np.asarray(x).astype(np.float64)


B, N, DIN, DH, DOUT, DIM = 8, 1024, 512, 128, 128, 512
ALPHA = 3.0


def setup_inputs():
    s = mx_kscale(DIM)
    r = np.random.standard_normal
    return {"emb1": bf(r((N, DIM)) * s), "emb2": bf(r((N, DIM)) * s),
            "lin1_w": bf(r((DIM, DIM)) * 0.05 / np.sqrt(DIM) / s[:, None]), "lin1_b": bf(r(DIM) * 0.02),
            "lin2_w": bf(r((DIM, DIM)) * 0.05 / np.sqrt(DIM) / s[:, None]), "lin2_b": bf(r(DIM) * 0.02)}


def reference(emb1, emb2, lin1_w, lin1_b, lin2_w, lin2_b):
    n1 = np.tanh(ALPHA * ((mxq(f64(emb1), 1, "e4m3") @ mxq(f64(lin1_w), 0, "e4m3")) + f64(lin1_b)))
    n2 = np.tanh(ALPHA * ((mxq(f64(emb2), 1, "e4m3") @ mxq(f64(lin2_w), 0, "e4m3")) + f64(lin2_b)))
    n1q = mxq(n1, 1, "e4m3")
    n2q = mxq(n2, 1, "e4m3")
    a = (n1q @ n2q.T) - (n2q @ n1q.T)
    return np.maximum(np.tanh(ALPHA * a), 0.0)

@@ -1,0 +1,205 @@
+import concourse.mybir as mybir
+from concourse.masks import make_identity
+
+FP8X4 = mybir.dt.float8_e4m3fn_x4
+BF16 = mybir.dt.bfloat16
+F32 = mybir.dt.float32
+U32 = mybir.dt.uint32
+U8 = mybir.dt.uint8
+TANH = mybir.ActivationFunctionType.Tanh
+
+P = 128
+PACK = 4
+NODES = 1024
+DIM = 512
+ALPHA = 3.0
+CHUNK = 512
+CHUNKS = NODES // CHUNK
+TILES_PER_CHUNK = CHUNK // P
+WORDS = DIM // 2
+BANK_NODES = 256
+
+FLOPS = 2 * (2 * NODES * DIM * DIM) + 2 * (2 * NODES * NODES * DIM)
+
+
+def quantise(nc, keep, grouped, width, name):
+    codes = keep.tile([P, width], U32, name="codes_" + name, align_bytes=64)
+    scales = keep.tile([P, width], U8, name="scales_" + name, align_bytes=64)
+    nc.vector.quantize_mx(out=codes[:].bitcast(FP8X4), scales=scales[:], in_=grouped[:])
+    return codes, scales
+
+
+def tile_gcn_pa_kernel(tc, emb1, emb2, lin1_w, lin1_b, lin2_w, lin2_b, out):
+    nc = tc.nc
+    embs = (emb1, emb2)
+    weights = (lin1_w, lin2_w)
+    biases = (lin1_b, lin2_b)
+    sides = range(2)
+
+    with tc.tile_pool(name="keep", bufs=1) as keep, tc.psum_pool(name="psum", bufs=8) as psum:
+
+        w_raw = {}
+        emb_raw = {}
+
+        def load_weight(s):
+            w_raw[s] = keep.tile([P, PACK * DIM], BF16, name="w_raw_%d" % s)
+            nc.sync.dma_start(
+                out=w_raw[s][:].rearrange("p (u ec) -> p u ec", u=2),
+                in_=weights[s].rearrange("(u p e) c -> p u (e c)", u=2, e=2),
+            )
+
+        def load_chunk(s, h):
+            emb_raw[s, h] = keep.tile([P, TILES_PER_CHUNK * DIM], BF16, name="emb_raw_%d_%d" % (s, h))
+            nc.sync.dma_start(
+                out=emb_raw[s, h][:].rearrange("p (r k) -> p r k", r=TILES_PER_CHUNK),
+                in_=embs[s][h * CHUNK : (h + 1) * CHUNK, :].rearrange("(r p) k -> p r k", p=P),
+            )
+
+        load_weight(1)
+        load_chunk(1, 0)
+        load_weight(0)
+        load_chunk(0, 0)
+        load_chunk(1, 1)
+        load_chunk(0, 1)
+
+        bias3 = {}
+        for s in sides:
+            bias_raw = keep.tile([P, PACK], BF16, name="bias_raw_%d" % s)
+            nc.scalar.dma_start(out=bias_raw[:], in_=biases[s].rearrange("(p j) -> p j", j=PACK))
+            bias3[s] = keep.tile([P, PACK], F32, name="bias3_%d" % s)
+            nc.vector.tensor_scalar_mul(bias3[s][:], bias_raw[:], ALPHA)
+
+        identity = keep.tile([P, P], F32, name="identity")
+        make_identity(nc, identity[:])
+
+        zero = keep.tile([P, 1], F32, name="zero")
+        warm = keep.tile([P, 1], F32, name="warm")
+        nc.vector.memset(zero[:], 0.0)
+        nc.scalar.activation(out=warm[:], in_=zero[:], func=TANH)
+
+        w_mx = {}
+        emb_mx = {}
+
+        def quantise_weight(s):
+            grouped = keep.tile([P, DIM * PACK], BF16, name="w_grouped_%d" % s, align_bytes=64)
+            nc.vector.tensor_copy(
+                out=grouped[:].rearrange("p (j q t) -> p q t j", j=PACK, t=PACK),
+                in_=w_raw[s][:].rearrange("p (t q j) -> p q t j", t=PACK, j=PACK),
+            )
+            w_mx[s] = quantise(nc, keep, grouped, DIM, "w_%d" % s)
+
+        def quantise_chunk(s, h):
+            words = emb_raw[s, h][:].bitcast(F32)
+            grouped = keep.tile([P, CHUNK * PACK], BF16, name="emb_grouped_%d_%d" % (s, h), align_bytes=64)
+            grouped_words = grouped[:].bitcast(F32).rearrange("p (n u) -> p n u", u=2)
+            for b in range(CHUNK // BANK_NODES):
+                flipped = psum.tile([P, 2, BANK_NODES], F32, tag="bank")
+                for r in range(BANK_NODES // P):
+                    first_word = (b * (BANK_NODES // P) + r) * WORDS
+                    for u in range(2):
+                        nc.tensor.transpose(
+                            flipped[:, u, r * P : (r + 1) * P],
+                            words[:, first_word + u * P : first_word + (u + 1) * P],
+                            identity[:],
+                        )
+                dst = grouped_words[:, b * BANK_NODES : (b + 1) * BANK_NODES, :]
+                src = flipped[:].rearrange("p u n -> p n u")
+                if b % 2 == 0:
+                    nc.vector.tensor_copy(out=dst, in_=src)
+                else:
+                    nc.scalar.copy(out=dst, in_=src)
+            emb_mx[s, h] = quantise(nc, keep, grouped, CHUNK, "emb_%d_%d" % (s, h))
+
+        n_planes = {}
+        n_mx = {}
+        minus_n2_mx = {}
+
+        def first_stage(s, h):
+            w_codes, w_scales = w_mx[s]
+            emb_codes, emb_scales = emb_mx[s, h]
+            n_planes[s, h] = keep.tile([P, PACK * CHUNK], BF16, name="n_planes_%d_%d" % (s, h))
+            for j in range(PACK):
+                cols = slice(j * P, (j + 1) * P)
+                acc = psum.tile([P, CHUNK], F32, tag="bank")
+                nc.tensor.matmul_mx(
+                    out=acc[:],
+                    lhsT=w_codes[:, cols].bitcast(FP8X4),
+                    lhsT_scale=w_scales[:, cols],
+                    rhs=emb_codes[:].bitcast(FP8X4),
+                    rhs_scale=emb_scales[:],
+                    start=True,
+                    stop=True,
+                )
+                nc.scalar.activation(
+                    out=n_planes[s, h][:, j * CHUNK : (j + 1) * CHUNK],
+                    in_=acc[:],
+                    func=TANH,
+                    bias=bias3[s][:, j : j + 1],
+                    scale=ALPHA,
+                )
+
+        def quantise_features(s, h):
+            grouped = keep.tile([P, CHUNK * PACK], BF16, name="n_grouped_%d_%d" % (s, h), align_bytes=64)
+            nc.vector.tensor_copy(
+                out=grouped[:].rearrange("p (c i j) -> p c j i", i=4, j=PACK),
+                in_=n_planes[s, h][:].rearrange("p (j c i) -> p c j i", j=PACK, i=4),
+            )
+            n_mx[s, h] = quantise(nc, keep, grouped, CHUNK, "n_%d_%d" % (s, h))
+            if s == 1:
+                negated = keep.tile([P, CHUNK * PACK], BF16, name="n_negated_%d" % h, align_bytes=64)
+                nc.vector.tensor_scalar_mul(negated[:], grouped[:], -1.0)
+                minus_n2_mx[h] = quantise(nc, keep, negated, CHUNK, "minus_n2_%d" % h)
+
+        def second_stage(row_chunk, col_chunk):
+            n1_row_codes, n1_row_scales = n_mx[0, row_chunk]
+            m2_row_codes, m2_row_scales = minus_n2_mx[row_chunk]
+            n1_col_codes, n1_col_scales = n_mx[0, col_chunk]
+            n2_col_codes, n2_col_scales = n_mx[1, col_chunk]
+            for r in range(TILES_PER_CHUNK):
+                rows = slice(r * P, (r + 1) * P)
+                acc = psum.tile([P, CHUNK], F32, tag="bank")
+                nc.tensor.matmul_mx(
+                    out=acc[:],
+                    lhsT=n1_row_codes[:, rows].bitcast(FP8X4),
+                    lhsT_scale=n1_row_scales[:, rows],
+                    rhs=n2_col_codes[:].bitcast(FP8X4),
+                    rhs_scale=n2_col_scales[:],
+                    start=True,
+                    stop=False,
+                )
+                nc.tensor.matmul_mx(
+                    out=acc[:],
+                    lhsT=m2_row_codes[:, rows].bitcast(FP8X4),
+                    lhsT_scale=m2_row_scales[:, rows],
+                    rhs=n1_col_codes[:].bitcast(FP8X4),
+                    rhs_scale=n1_col_scales[:],
+                    start=False,
+                    stop=True,
+                )
+                block = keep.tile([P, CHUNK], F32, name="block_%d_%d_%d" % (row_chunk, r, col_chunk))
+                nc.scalar.activation(out=block[:], in_=acc[:], func=TANH, scale=ALPHA)
+                nc.vector.tensor_scalar_max(block[:], block[:], 0.0)
+                first_row = row_chunk * CHUNK + r * P
+                nc.sync.dma_start(
+                    out=out[first_row : first_row + P, col_chunk * CHUNK : (col_chunk + 1) * CHUNK],
+                    in_=block[:],
+                )
+
+        quantise_weight(1)
+        quantise_chunk(1, 0)
+        quantise_weight(0)
+        quantise_chunk(0, 0)
+        first_stage(1, 0)
+        first_stage(0, 0)
+        quantise_chunk(1, 1)
+        quantise_chunk(0, 1)
+        quantise_features(1, 0)
+        quantise_features(0, 0)
+        second_stage(0, 0)
+        first_stage(1, 1)
+        first_stage(0, 1)
+        quantise_features(1, 1)
+        quantise_features(0, 1)
+        second_stage(0, 1)
+        second_stage(1, 0)
+        second_stage(1, 1)

@@ -13,20 +13,14 @@ PACK = 4
 NODES = 1024
 DIM = 512
 ALPHA = 3.0
-CHUNK = 512
+CHUNK = 256
 CHUNKS = NODES // CHUNK
-TILES_PER_CHUNK = CHUNK // P
+TILES = CHUNK // P
 WORDS = DIM // 2
-BANK_NODES = 256
+AHEAD = 3
+BLOCKS_AFTER = 2
 
 FLOPS = 2 * (2 * NODES * DIM * DIM) + 2 * (2 * NODES * NODES * DIM)
-
-
-def quantise(nc, keep, grouped, width, name):
-    codes = keep.tile([P, width], U32, name="codes_" + name, align_bytes=64)
-    scales = keep.tile([P, width], U8, name="scales_" + name, align_bytes=64)
-    nc.vector.quantize_mx(out=codes[:].bitcast(FP8X4), scales=scales[:], in_=grouped[:])
-    return codes, scales
 
 
 def tile_gcn_pa_kernel(tc, emb1, emb2, lin1_w, lin1_b, lin2_w, lin2_b, out):
@@ -34,40 +28,45 @@ def tile_gcn_pa_kernel(tc, emb1, emb2, lin1_w, lin1_b, lin2_w, lin2_b, out):
     embs = (emb1, emb2)
     weights = (lin1_w, lin2_w)
     biases = (lin1_b, lin2_b)
-    sides = range(2)
+    units = [(side, chunk) for chunk in range(CHUNKS) for side in (1, 0)]
 
-    with tc.tile_pool(name="keep", bufs=1) as keep, tc.psum_pool(name="psum", bufs=8) as psum:
+    with tc.tile_pool(name="keep", bufs=1) as keep, tc.psum_pool(name="psum", bufs=8) as psum, tc.manual_schedule():
+
+        def quantise(grouped, width, name):
+            codes = keep.tile([P, width], U32, name="codes_" + name, align_bytes=64)
+            scales = keep.tile([P, width], U8, name="scales_" + name, align_bytes=64)
+            nc.vector.quantize_mx(out=codes[:].bitcast(FP8X4), scales=scales[:], in_=grouped[:])
+            return codes, scales
 
         w_raw = {}
         emb_raw = {}
 
-        def load_weight(s):
-            w_raw[s] = keep.tile([P, PACK * DIM], BF16, name="w_raw_%d" % s)
+        def load_weight(side):
+            w_raw[side] = keep.tile([P, PACK * DIM], BF16, name="w_raw_%d" % side)
             nc.sync.dma_start(
-                out=w_raw[s][:].rearrange("p (u ec) -> p u ec", u=2),
-                in_=weights[s].rearrange("(u p e) c -> p u (e c)", u=2, e=2),
+                out=w_raw[side][:].rearrange("p (u ec) -> p u ec", u=2),
+                in_=weights[side].rearrange("(u p e) c -> p u (e c)", u=2, e=2),
             )
 
-        def load_chunk(s, h):
-            emb_raw[s, h] = keep.tile([P, TILES_PER_CHUNK * DIM], BF16, name="emb_raw_%d_%d" % (s, h))
+        def load_unit(unit):
+            side, chunk = unit
+            emb_raw[unit] = keep.tile([P, TILES * DIM], BF16, name="emb_raw_%d_%d" % unit)
             nc.sync.dma_start(
-                out=emb_raw[s, h][:].rearrange("p (r k) -> p r k", r=TILES_PER_CHUNK),
-                in_=embs[s][h * CHUNK : (h + 1) * CHUNK, :].rearrange("(r p) k -> p r k", p=P),
+                out=emb_raw[unit][:].rearrange("p (r k) -> p r k", r=TILES),
+                in_=embs[side][chunk * CHUNK : (chunk + 1) * CHUNK, :].rearrange("(r p) k -> p r k", p=P),
             )
 
+        load_unit(units[0])
         load_weight(1)
-        load_chunk(1, 0)
+        load_unit(units[1])
         load_weight(0)
-        load_chunk(0, 0)
-        load_chunk(1, 1)
-        load_chunk(0, 1)
+        for unit in units[2:]:
+            load_unit(unit)
 
-        bias3 = {}
-        for s in sides:
-            bias_raw = keep.tile([P, PACK], BF16, name="bias_raw_%d" % s)
-            nc.scalar.dma_start(out=bias_raw[:], in_=biases[s].rearrange("(p j) -> p j", j=PACK))
-            bias3[s] = keep.tile([P, PACK], F32, name="bias3_%d" % s)
-            nc.vector.tensor_scalar_mul(bias3[s][:], bias_raw[:], ALPHA)
+        bias_raw = {}
+        for side in (1, 0):
+            bias_raw[side] = keep.tile([P, PACK], BF16, name="bias_raw_%d" % side)
+            nc.scalar.dma_start(out=bias_raw[side][:], in_=biases[side].rearrange("(p j) -> p j", j=PACK))
 
         identity = keep.tile([P, P], F32, name="identity")
         make_identity(nc, identity[:])
@@ -78,88 +77,103 @@ def tile_gcn_pa_kernel(tc, emb1, emb2, lin1_w, lin1_b, lin2_w, lin2_b, out):
         nc.scalar.activation(out=warm[:], in_=zero[:], func=TANH)
 
         w_mx = {}
+        bias3 = {}
         emb_mx = {}
 
-        def quantise_weight(s):
-            grouped = keep.tile([P, DIM * PACK], BF16, name="w_grouped_%d" % s, align_bytes=64)
+        w_grouped = {}
+
+        def regroup_weight(side):
+            w_grouped[side] = keep.tile([P, DIM * PACK], BF16, name="w_grouped_%d" % side, align_bytes=64)
             nc.vector.tensor_copy(
-                out=grouped[:].rearrange("p (j q t) -> p q t j", j=PACK, t=PACK),
-                in_=w_raw[s][:].rearrange("p (t q j) -> p q t j", t=PACK, j=PACK),
+                out=w_grouped[side][:].rearrange("p (j q t) -> p q t j", j=PACK, t=PACK),
+                in_=w_raw[side][:].rearrange("p (t q j) -> p q t j", t=PACK, j=PACK),
             )
-            w_mx[s] = quantise(nc, keep, grouped, DIM, "w_%d" % s)
+            bias3[side] = keep.tile([P, PACK], F32, name="bias3_%d" % side)
+            nc.vector.tensor_scalar_mul(bias3[side][:], bias_raw[side][:], ALPHA)
 
-        def quantise_chunk(s, h):
-            words = emb_raw[s, h][:].bitcast(F32)
-            grouped = keep.tile([P, CHUNK * PACK], BF16, name="emb_grouped_%d_%d" % (s, h), align_bytes=64)
-            grouped_words = grouped[:].bitcast(F32).rearrange("p (n u) -> p n u", u=2)
-            for b in range(CHUNK // BANK_NODES):
-                flipped = psum.tile([P, 2, BANK_NODES], F32, tag="bank")
-                for r in range(BANK_NODES // P):
-                    first_word = (b * (BANK_NODES // P) + r) * WORDS
-                    for u in range(2):
-                        nc.tensor.transpose(
-                            flipped[:, u, r * P : (r + 1) * P],
-                            words[:, first_word + u * P : first_word + (u + 1) * P],
-                            identity[:],
-                        )
-                dst = grouped_words[:, b * BANK_NODES : (b + 1) * BANK_NODES, :]
-                src = flipped[:].rearrange("p u n -> p n u")
-                if b % 2 == 0:
-                    nc.vector.tensor_copy(out=dst, in_=src)
-                else:
-                    nc.scalar.copy(out=dst, in_=src)
-            emb_mx[s, h] = quantise(nc, keep, grouped, CHUNK, "emb_%d_%d" % (s, h))
+        def quantise_weight(side):
+            w_mx[side] = quantise(w_grouped[side], DIM, "w_%d" % side)
 
-        n_planes = {}
+        emb_grouped = {}
+
+        def flip(unit):
+            words = emb_raw[unit][:].bitcast(F32)
+            flipped = psum.tile([P, 2, CHUNK], F32, tag="bank")
+            for r in range(TILES):
+                for u in range(2):
+                    nc.tensor.transpose(
+                        flipped[:, u, r * P : (r + 1) * P],
+                        words[:, r * WORDS + u * P : r * WORDS + (u + 1) * P],
+                        identity[:],
+                    )
+            emb_grouped[unit] = keep.tile([P, CHUNK * PACK], BF16, name="emb_grouped_%d_%d" % unit, align_bytes=64)
+            nc.scalar.copy(
+                out=emb_grouped[unit][:].bitcast(F32).rearrange("p (n u) -> p n u", u=2),
+                in_=flipped[:].rearrange("p u n -> p n u"),
+            )
+
+        def quantise_emb(unit):
+            emb_mx[unit] = quantise(emb_grouped[unit], CHUNK, "emb_%d_%d" % unit)
+
+        def prepare(unit):
+            flip(unit)
+            quantise_emb(unit)
+
+        n_grouped = {}
         n_mx = {}
         minus_n2_mx = {}
 
-        def first_stage(s, h):
-            w_codes, w_scales = w_mx[s]
-            emb_codes, emb_scales = emb_mx[s, h]
-            n_planes[s, h] = keep.tile([P, PACK * CHUNK], BF16, name="n_planes_%d_%d" % (s, h))
-            for j in range(PACK):
-                cols = slice(j * P, (j + 1) * P)
-                acc = psum.tile([P, CHUNK], F32, tag="bank")
-                nc.tensor.matmul_mx(
-                    out=acc[:],
-                    lhsT=w_codes[:, cols].bitcast(FP8X4),
-                    lhsT_scale=w_scales[:, cols],
-                    rhs=emb_codes[:].bitcast(FP8X4),
-                    rhs_scale=emb_scales[:],
-                    start=True,
-                    stop=True,
-                )
-                nc.scalar.activation(
-                    out=n_planes[s, h][:, j * CHUNK : (j + 1) * CHUNK],
-                    in_=acc[:],
-                    func=TANH,
-                    bias=bias3[s][:, j : j + 1],
-                    scale=ALPHA,
-                )
-
-        def quantise_features(s, h):
-            grouped = keep.tile([P, CHUNK * PACK], BF16, name="n_grouped_%d_%d" % (s, h), align_bytes=64)
+        def features(unit):
+            side = unit[0]
+            w_codes, w_scales = w_mx[side]
+            emb_codes, emb_scales = emb_mx[unit]
+            n_planes = keep.tile([P, PACK * CHUNK], BF16, name="n_planes_%d_%d" % unit)
+            for half in range(2):
+                acc = psum.tile([P, 2, CHUNK], F32, tag="bank")
+                for i in range(2):
+                    cols = slice((2 * half + i) * P, (2 * half + i + 1) * P)
+                    nc.tensor.matmul_mx(
+                        out=acc[:, i, :],
+                        lhsT=w_codes[:, cols].bitcast(FP8X4),
+                        lhsT_scale=w_scales[:, cols],
+                        rhs=emb_codes[:].bitcast(FP8X4),
+                        rhs_scale=emb_scales[:],
+                        start=True,
+                        stop=True,
+                    )
+                for i in range(2):
+                    j = 2 * half + i
+                    nc.scalar.activation(
+                        out=n_planes[:, j * CHUNK : (j + 1) * CHUNK],
+                        in_=acc[:, i, :],
+                        func=TANH,
+                        bias=bias3[side][:, j : j + 1],
+                        scale=ALPHA,
+                    )
+            n_grouped[unit] = keep.tile([P, CHUNK * PACK], BF16, name="n_grouped_%d_%d" % unit, align_bytes=64)
             nc.vector.tensor_copy(
-                out=grouped[:].rearrange("p (c i j) -> p c j i", i=4, j=PACK),
-                in_=n_planes[s, h][:].rearrange("p (j c i) -> p c j i", j=PACK, i=4),
+                out=n_grouped[unit][:].rearrange("p (c i j) -> p c j i", i=4, j=PACK),
+                in_=n_planes[:].rearrange("p (j c i) -> p c j i", j=PACK, i=4),
             )
-            n_mx[s, h] = quantise(nc, keep, grouped, CHUNK, "n_%d_%d" % (s, h))
-            if s == 1:
-                negated = keep.tile([P, CHUNK * PACK], BF16, name="n_negated_%d" % h, align_bytes=64)
-                nc.vector.tensor_scalar_mul(negated[:], grouped[:], -1.0)
-                minus_n2_mx[h] = quantise(nc, keep, negated, CHUNK, "minus_n2_%d" % h)
 
-        def second_stage(row_chunk, col_chunk):
+        def quantise_features(unit):
+            n_mx[unit] = quantise(n_grouped[unit], CHUNK, "n_%d_%d" % unit)
+
+        def negate_n2(chunk):
+            negated = keep.tile([P, CHUNK * PACK], BF16, name="n_negated_%d" % chunk, align_bytes=64)
+            nc.vector.tensor_scalar_mul(negated[:], n_grouped[1, chunk][:], -1.0)
+            return negated
+
+        def block(row_chunk, col_chunk):
             n1_row_codes, n1_row_scales = n_mx[0, row_chunk]
             m2_row_codes, m2_row_scales = minus_n2_mx[row_chunk]
             n1_col_codes, n1_col_scales = n_mx[0, col_chunk]
             n2_col_codes, n2_col_scales = n_mx[1, col_chunk]
-            for r in range(TILES_PER_CHUNK):
+            acc = psum.tile([P, TILES, CHUNK], F32, tag="bank")
+            for r in range(TILES):
                 rows = slice(r * P, (r + 1) * P)
-                acc = psum.tile([P, CHUNK], F32, tag="bank")
                 nc.tensor.matmul_mx(
-                    out=acc[:],
+                    out=acc[:, r, :],
                     lhsT=n1_row_codes[:, rows].bitcast(FP8X4),
                     lhsT_scale=n1_row_scales[:, rows],
                     rhs=n2_col_codes[:].bitcast(FP8X4),
@@ -168,7 +182,7 @@ def tile_gcn_pa_kernel(tc, emb1, emb2, lin1_w, lin1_b, lin2_w, lin2_b, out):
                     stop=False,
                 )
                 nc.tensor.matmul_mx(
-                    out=acc[:],
+                    out=acc[:, r, :],
                     lhsT=m2_row_codes[:, rows].bitcast(FP8X4),
                     lhsT_scale=m2_row_scales[:, rows],
                     rhs=n1_col_codes[:].bitcast(FP8X4),
@@ -176,30 +190,40 @@ def tile_gcn_pa_kernel(tc, emb1, emb2, lin1_w, lin1_b, lin2_w, lin2_b, out):
                     start=False,
                     stop=True,
                 )
-                block = keep.tile([P, CHUNK], F32, name="block_%d_%d_%d" % (row_chunk, r, col_chunk))
-                nc.scalar.activation(out=block[:], in_=acc[:], func=TANH, scale=ALPHA)
-                nc.vector.tensor_scalar_max(block[:], block[:], 0.0)
-                first_row = row_chunk * CHUNK + r * P
-                nc.sync.dma_start(
-                    out=out[first_row : first_row + P, col_chunk * CHUNK : (col_chunk + 1) * CHUNK],
-                    in_=block[:],
-                )
+            result = keep.tile([P, TILES, CHUNK], F32, name="result_%d_%d" % (row_chunk, col_chunk))
+            nc.scalar.activation(out=result[:], in_=acc[:], func=TANH, scale=ALPHA)
+            nc.vector.tensor_scalar_max(result[:], result[:], 0.0)
+            nc.sync.dma_start(
+                out=out[
+                    row_chunk * CHUNK : (row_chunk + 1) * CHUNK, col_chunk * CHUNK : (col_chunk + 1) * CHUNK
+                ].rearrange("(r p) n -> p r n", p=P),
+                in_=result[:],
+            )
 
-        quantise_weight(1)
-        quantise_chunk(1, 0)
-        quantise_weight(0)
-        quantise_chunk(0, 0)
-        first_stage(1, 0)
-        first_stage(0, 0)
-        quantise_chunk(1, 1)
-        quantise_chunk(0, 1)
-        quantise_features(1, 0)
-        quantise_features(0, 0)
-        second_stage(0, 0)
-        first_stage(1, 1)
-        first_stage(0, 1)
-        quantise_features(1, 1)
-        quantise_features(0, 1)
-        second_stage(0, 1)
-        second_stage(1, 0)
-        second_stage(1, 1)
+        def blocks_of(chunk):
+            for earlier in range(chunk):
+                block(earlier, chunk)
+            for col_chunk in range(chunk + 1):
+                block(chunk, col_chunk)
+
+        for unit in units[:2]:
+            flip(unit)
+            regroup_weight(unit[0])
+            quantise_emb(unit)
+            quantise_weight(unit[0])
+        for unit in units[2:AHEAD]:
+            prepare(unit)
+        for step in range(len(units) + BLOCKS_AFTER):
+            if step < len(units):
+                unit = units[step]
+                side, chunk = unit
+                features(unit)
+                if side == 0:
+                    negated = negate_n2(chunk)
+                if step + AHEAD < len(units):
+                    prepare(units[step + AHEAD])
+                quantise_features(unit)
+                if side == 0:
+                    minus_n2_mx[chunk] = quantise(negated, CHUNK, "minus_n2_%d" % chunk)
+            if step >= 1 + BLOCKS_AFTER and (step - 1 - BLOCKS_AFTER) % 2 == 0:
+                blocks_of((step - 1 - BLOCKS_AFTER) // 2)

@@ -82,17 +82,29 @@ def tile_gcn_pa_kernel(tc, emb1, emb2, lin1_w, lin1_b, lin2_w, lin2_b, out):
 
         w_grouped = {}
 
-        def regroup_weight(side):
+        def regroup_weight(side, half, copy):
+            tiles = slice(2 * half, 2 * half + 2)
+            copy(
+                out=w_grouped[side][:].rearrange("p (j q t) -> p q t j", j=PACK, t=PACK)[:, :, :, tiles],
+                in_=w_raw[side][:].rearrange("p (t q j) -> p q t j", t=PACK, j=PACK)[:, :, :, tiles],
+            )
+
+        def quantise_weight(side, half):
+            codes, scales = w_mx[side]
+            cols = slice(half * DIM // 2, (half + 1) * DIM // 2)
+            nc.vector.quantize_mx(
+                out=codes[:, cols].bitcast(FP8X4),
+                scales=scales[:, cols],
+                in_=w_grouped[side][:, half * DIM * PACK // 2 : (half + 1) * DIM * PACK // 2],
+            )
+
+        for side in (1, 0):
             w_grouped[side] = keep.tile([P, DIM * PACK], BF16, name="w_grouped_%d" % side, align_bytes=64)
-            nc.vector.tensor_copy(
-                out=w_grouped[side][:].rearrange("p (j q t) -> p q t j", j=PACK, t=PACK),
-                in_=w_raw[side][:].rearrange("p (t q j) -> p q t j", t=PACK, j=PACK),
+            w_mx[side] = (
+                keep.tile([P, DIM], U32, name="codes_w_%d" % side, align_bytes=64),
+                keep.tile([P, DIM], U8, name="scales_w_%d" % side, align_bytes=64),
             )
             bias3[side] = keep.tile([P, PACK], F32, name="bias3_%d" % side)
-            nc.vector.tensor_scalar_mul(bias3[side][:], bias_raw[side][:], ALPHA)
-
-        def quantise_weight(side):
-            w_mx[side] = quantise(w_grouped[side], DIM, "w_%d" % side)
 
         emb_grouped = {}
 
@@ -107,17 +119,14 @@ def tile_gcn_pa_kernel(tc, emb1, emb2, lin1_w, lin1_b, lin2_w, lin2_b, out):
                         identity[:],
                     )
             emb_grouped[unit] = keep.tile([P, CHUNK * PACK], BF16, name="emb_grouped_%d_%d" % unit, align_bytes=64)
-            nc.scalar.copy(
+            copy_out = nc.scalar.copy if unit[0] == 1 else nc.vector.tensor_copy
+            copy_out(
                 out=emb_grouped[unit][:].bitcast(F32).rearrange("p (n u) -> p n u", u=2),
                 in_=flipped[:].rearrange("p u n -> p n u"),
             )
 
         def quantise_emb(unit):
             emb_mx[unit] = quantise(emb_grouped[unit], CHUNK, "emb_%d_%d" % unit)
-
-        def prepare(unit):
-            flip(unit)
-            quantise_emb(unit)
 
         n_grouped = {}
         n_mx = {}
@@ -200,30 +209,50 @@ def tile_gcn_pa_kernel(tc, emb1, emb2, lin1_w, lin1_b, lin2_w, lin2_b, out):
                 in_=result[:],
             )
 
-        def blocks_of(chunk):
-            for earlier in range(chunk):
-                block(earlier, chunk)
-            for col_chunk in range(chunk + 1):
-                block(chunk, col_chunk)
+        blocks = []
+        for chunk in range(CHUNKS):
+            blocks.extend([(earlier, chunk) for earlier in range(chunk)])
+            blocks.extend([(chunk, col_chunk) for col_chunk in range(chunk + 1)])
+        issued = [0]
 
-        for unit in units[:2]:
-            flip(unit)
-            regroup_weight(unit[0])
-            quantise_emb(unit)
-            quantise_weight(unit[0])
-        for unit in units[2:AHEAD]:
-            prepare(unit)
-        for step in range(len(units) + BLOCKS_AFTER):
-            if step < len(units):
-                unit = units[step]
-                side, chunk = unit
-                features(unit)
-                if side == 0:
-                    negated = negate_n2(chunk)
-                if step + AHEAD < len(units):
-                    prepare(units[step + AHEAD])
-                quantise_features(unit)
-                if side == 0:
-                    minus_n2_mx[chunk] = quantise(negated, CHUNK, "minus_n2_%d" % chunk)
-            if step >= 1 + BLOCKS_AFTER and (step - 1 - BLOCKS_AFTER) % 2 == 0:
-                blocks_of((step - 1 - BLOCKS_AFTER) // 2)
+        def one_block(step):
+            if issued[0] < len(blocks) and step >= 2 * max(blocks[issued[0]]) + 1 + BLOCKS_AFTER:
+                block(*blocks[issued[0]])
+                issued[0] = issued[0] + 1
+
+        flip(units[0])
+        regroup_weight(1, 0, nc.vector.tensor_copy)
+        regroup_weight(1, 1, nc.scalar.copy)
+        for side in (1, 0):
+            nc.vector.tensor_scalar_mul(bias3[side][:], bias_raw[side][:], ALPHA)
+        quantise_emb(units[0])
+        quantise_weight(1, 0)
+        flip(units[1])
+        quantise_weight(1, 1)
+        quantise_emb(units[1])
+        regroup_weight(0, 0, nc.vector.tensor_copy)
+        regroup_weight(0, 1, nc.vector.tensor_copy)
+        quantise_weight(0, 0)
+        quantise_weight(0, 1)
+
+        prepared = 2
+        for step in range(len(units)):
+            unit = units[step]
+            side, chunk = unit
+            features(unit)
+            one_block(step)
+            if side == 0:
+                negated = negate_n2(chunk)
+            flipped_now = units[prepared : step + AHEAD + 1]
+            prepared = prepared + len(flipped_now)
+            for later in flipped_now:
+                flip(later)
+            one_block(step)
+            quantise_features(unit)
+            for later in flipped_now:
+                quantise_emb(later)
+            one_block(step)
+            if side == 0:
+                minus_n2_mx[chunk] = quantise(negated, CHUNK, "minus_n2_%d" % chunk)
+        for row_chunk, col_chunk in blocks[issued[0] :]:
+            block(row_chunk, col_chunk)

@@ -16,6 +16,7 @@ ALPHA = 3.0
 CHUNK = 256
 CHUNKS = NODES // CHUNK
 TILES = CHUNK // P
+BANK = 512
 WORDS = DIM // 2
 AHEAD = 3
 BLOCKS_AFTER = 2
@@ -75,6 +76,14 @@ def tile_gcn_pa_kernel(tc, emb1, emb2, lin1_w, lin1_b, lin2_w, lin2_b, out):
         warm = keep.tile([P, 1], F32, name="warm")
         nc.vector.memset(zero[:], 0.0)
         nc.scalar.activation(out=warm[:], in_=zero[:], func=TANH)
+
+        idle = keep.tile([P, BANK], BF16, name="idle")
+        nc.vector.memset(idle[:], 0.0)
+
+        def keep_busy(times):
+            for i in range(times):
+                unread = psum.tile([P, BANK], F32, tag="bank")
+                nc.tensor.matmul(unread[:], lhsT=idle[:, :P], rhs=idle[:], start=True, stop=True)
 
         w_mx = {}
         bias3 = {}
@@ -220,7 +229,9 @@ def tile_gcn_pa_kernel(tc, emb1, emb2, lin1_w, lin1_b, lin2_w, lin2_b, out):
                 block(*blocks[issued[0]])
                 issued[0] = issued[0] + 1
 
+        keep_busy(3)
         flip(units[0])
+        keep_busy(2)
         regroup_weight(1, 0, nc.vector.tensor_copy)
         regroup_weight(1, 1, nc.scalar.copy)
         for side in (1, 0):

@@ -13,13 +13,8 @@ PACK = 4
 NODES = 1024
 DIM = 512
 ALPHA = 3.0
-CHUNK = 256
-CHUNKS = NODES // CHUNK
-TILES = CHUNK // P
 BANK = 512
 WORDS = DIM // 2
-AHEAD = 3
-BLOCKS_AFTER = 2
 
 FLOPS = 2 * (2 * NODES * DIM * DIM) + 2 * (2 * NODES * NODES * DIM)
 
@@ -29,15 +24,12 @@ def tile_gcn_pa_kernel(tc, emb1, emb2, lin1_w, lin1_b, lin2_w, lin2_b, out):
     embs = (emb1, emb2)
     weights = (lin1_w, lin2_w)
     biases = (lin1_b, lin2_b)
-    units = [(side, chunk) for chunk in range(CHUNKS) for side in (1, 0)]
+    units = [(1, 0, 256), (1, 256, 256), (0, 0, 256), (0, 256, 256), (1, 512, 256), (0, 512, 256), (1, 768, 256), (0, 768, 256)]
 
     with tc.tile_pool(name="keep", bufs=1) as keep, tc.psum_pool(name="psum", bufs=8) as psum, tc.manual_schedule():
 
-        def quantise(grouped, width, name):
-            codes = keep.tile([P, width], U32, name="codes_" + name, align_bytes=64)
-            scales = keep.tile([P, width], U8, name="scales_" + name, align_bytes=64)
-            nc.vector.quantize_mx(out=codes[:].bitcast(FP8X4), scales=scales[:], in_=grouped[:])
-            return codes, scales
+        def quantise(codes, scales, cols, grouped):
+            nc.vector.quantize_mx(out=codes[:, cols].bitcast(FP8X4), scales=scales[:, cols], in_=grouped)
 
         w_raw = {}
         emb_raw = {}
@@ -50,11 +42,11 @@ def tile_gcn_pa_kernel(tc, emb1, emb2, lin1_w, lin1_b, lin2_w, lin2_b, out):
             )
 
         def load_unit(unit):
-            side, chunk = unit
-            emb_raw[unit] = keep.tile([P, TILES * DIM], BF16, name="emb_raw_%d_%d" % unit)
+            side, first, nodes = unit
+            emb_raw[unit] = keep.tile([P, nodes // P * DIM], BF16, name="emb_raw_%d_%d" % (side, first))
             nc.sync.dma_start(
-                out=emb_raw[unit][:].rearrange("p (r k) -> p r k", r=TILES),
-                in_=embs[side][chunk * CHUNK : (chunk + 1) * CHUNK, :].rearrange("(r p) k -> p r k", p=P),
+                out=emb_raw[unit][:].rearrange("p (r k) -> p r k", k=DIM),
+                in_=embs[side][first : first + nodes, :].rearrange("(r p) k -> p r k", p=P),
             )
 
         load_unit(units[0])
@@ -85,185 +77,265 @@ def tile_gcn_pa_kernel(tc, emb1, emb2, lin1_w, lin1_b, lin2_w, lin2_b, out):
                 unread = psum.tile([P, BANK], F32, tag="bank")
                 nc.tensor.matmul(unread[:], lhsT=idle[:, :P], rhs=idle[:], start=True, stop=True)
 
-        w_mx = {}
-        bias3 = {}
-        emb_mx = {}
-
         w_grouped = {}
+        w_codes = {}
+        w_scales = {}
+        bias3 = {}
+        n_codes = {}
+        n_scales = {}
+        for side in (1, 0):
+            w_grouped[side] = keep.tile([P, DIM * PACK], BF16, name="w_grouped_%d" % side, align_bytes=64)
+            w_codes[side] = keep.tile([P, DIM], U32, name="codes_w_%d" % side, align_bytes=64)
+            w_scales[side] = keep.tile([P, DIM], U8, name="scales_w_%d" % side, align_bytes=64)
+            bias3[side] = keep.tile([P, PACK], F32, name="bias3_%d" % side)
+            n_codes[side] = keep.tile([P, NODES], U32, name="codes_n_%d" % side, align_bytes=64)
+            n_scales[side] = keep.tile([P, NODES], U8, name="scales_n_%d" % side, align_bytes=64)
+        minus_codes = keep.tile([P, NODES], U32, name="codes_minus", align_bytes=64)
+        minus_scales = keep.tile([P, NODES], U8, name="scales_minus", align_bytes=64)
 
-        def regroup_weight(side, half, copy):
+        def regroup_weight(side, half, engine="V"):
             tiles = slice(2 * half, 2 * half + 2)
+            copy = nc.scalar.copy if engine == "A" else nc.vector.tensor_copy
             copy(
                 out=w_grouped[side][:].rearrange("p (j q t) -> p q t j", j=PACK, t=PACK)[:, :, :, tiles],
                 in_=w_raw[side][:].rearrange("p (t q j) -> p q t j", t=PACK, j=PACK)[:, :, :, tiles],
             )
 
-        def quantise_weight(side, half):
-            codes, scales = w_mx[side]
-            cols = slice(half * DIM // 2, (half + 1) * DIM // 2)
-            nc.vector.quantize_mx(
-                out=codes[:, cols].bitcast(FP8X4),
-                scales=scales[:, cols],
-                in_=w_grouped[side][:, half * DIM * PACK // 2 : (half + 1) * DIM * PACK // 2],
-            )
+        def scale_biases():
+            for side in (1, 0):
+                nc.vector.tensor_scalar_mul(bias3[side][:], bias_raw[side][:], ALPHA)
 
-        for side in (1, 0):
-            w_grouped[side] = keep.tile([P, DIM * PACK], BF16, name="w_grouped_%d" % side, align_bytes=64)
-            w_mx[side] = (
-                keep.tile([P, DIM], U32, name="codes_w_%d" % side, align_bytes=64),
-                keep.tile([P, DIM], U8, name="scales_w_%d" % side, align_bytes=64),
+        def quantise_weight(side, half):
+            cols = slice(half * DIM // 2, (half + 1) * DIM // 2)
+            quantise(
+                w_codes[side],
+                w_scales[side],
+                cols,
+                w_grouped[side][:, half * DIM * PACK // 2 : (half + 1) * DIM * PACK // 2],
             )
-            bias3[side] = keep.tile([P, PACK], F32, name="bias3_%d" % side)
 
         emb_grouped = {}
+        emb_codes = {}
+        emb_scales = {}
+
+        flipped_of = {}
 
         def flip(unit):
+            side, first, nodes = unit
             words = emb_raw[unit][:].bitcast(F32)
-            flipped = psum.tile([P, 2, CHUNK], F32, tag="bank")
-            for r in range(TILES):
+            flipped_of[unit] = psum.tile([P, 2, nodes], F32, tag="bank", name="flipped_%d_%d" % (side, first))
+            for r in range(nodes // P):
                 for u in range(2):
                     nc.tensor.transpose(
-                        flipped[:, u, r * P : (r + 1) * P],
+                        flipped_of[unit][:, u, r * P : (r + 1) * P],
                         words[:, r * WORDS + u * P : r * WORDS + (u + 1) * P],
                         identity[:],
                     )
-            emb_grouped[unit] = keep.tile([P, CHUNK * PACK], BF16, name="emb_grouped_%d_%d" % unit, align_bytes=64)
-            copy_out = nc.scalar.copy if unit[0] == 1 else nc.vector.tensor_copy
-            copy_out(
+
+        def copy_flipped(unit, engine="A"):
+            side, first, nodes = unit
+            emb_grouped[unit] = keep.tile(
+                [P, nodes * PACK], BF16, name="emb_grouped_%d_%d" % (side, first), align_bytes=64
+            )
+            copy = nc.scalar.copy if engine == "A" else nc.vector.tensor_copy
+            copy(
                 out=emb_grouped[unit][:].bitcast(F32).rearrange("p (n u) -> p n u", u=2),
-                in_=flipped[:].rearrange("p u n -> p n u"),
+                in_=flipped_of[unit][:].rearrange("p u n -> p n u"),
             )
 
         def quantise_emb(unit):
-            emb_mx[unit] = quantise(emb_grouped[unit], CHUNK, "emb_%d_%d" % unit)
+            side, first, nodes = unit
+            emb_codes[unit] = keep.tile([P, nodes], U32, name="codes_emb_%d_%d" % (side, first), align_bytes=64)
+            emb_scales[unit] = keep.tile([P, nodes], U8, name="scales_emb_%d_%d" % (side, first), align_bytes=64)
+            quantise(emb_codes[unit], emb_scales[unit], slice(0, nodes), emb_grouped[unit][:])
 
+        n_planes = {}
         n_grouped = {}
-        n_mx = {}
-        minus_n2_mx = {}
+        n2_negated = {}
 
         def features(unit):
-            side = unit[0]
-            w_codes, w_scales = w_mx[side]
-            emb_codes, emb_scales = emb_mx[unit]
-            n_planes = keep.tile([P, PACK * CHUNK], BF16, name="n_planes_%d_%d" % unit)
-            for half in range(2):
-                acc = psum.tile([P, 2, CHUNK], F32, tag="bank")
-                for i in range(2):
-                    cols = slice((2 * half + i) * P, (2 * half + i + 1) * P)
+            side, first, nodes = unit
+            n_planes[unit] = keep.tile([P, PACK * nodes], BF16, name="n_planes_%d_%d" % (side, first))
+            per_bank = BANK // nodes
+            for j0 in range(0, PACK, per_bank):
+                acc = psum.tile([P, per_bank, nodes], F32, tag="bank")
+                for i in range(per_bank):
+                    cols = slice((j0 + i) * P, (j0 + i + 1) * P)
                     nc.tensor.matmul_mx(
                         out=acc[:, i, :],
-                        lhsT=w_codes[:, cols].bitcast(FP8X4),
-                        lhsT_scale=w_scales[:, cols],
-                        rhs=emb_codes[:].bitcast(FP8X4),
-                        rhs_scale=emb_scales[:],
+                        lhsT=w_codes[side][:, cols].bitcast(FP8X4),
+                        lhsT_scale=w_scales[side][:, cols],
+                        rhs=emb_codes[unit][:].bitcast(FP8X4),
+                        rhs_scale=emb_scales[unit][:],
                         start=True,
                         stop=True,
                     )
-                for i in range(2):
-                    j = 2 * half + i
+                for i in range(per_bank):
+                    j = j0 + i
                     nc.scalar.activation(
-                        out=n_planes[:, j * CHUNK : (j + 1) * CHUNK],
+                        out=n_planes[unit][:, j * nodes : (j + 1) * nodes],
                         in_=acc[:, i, :],
                         func=TANH,
                         bias=bias3[side][:, j : j + 1],
                         scale=ALPHA,
                     )
-            n_grouped[unit] = keep.tile([P, CHUNK * PACK], BF16, name="n_grouped_%d_%d" % unit, align_bytes=64)
+
+        def regroup_features(unit):
+            side, first, nodes = unit
+            n_grouped[unit] = keep.tile([P, nodes * PACK], BF16, name="n_grouped_%d_%d" % (side, first), align_bytes=64)
             nc.vector.tensor_copy(
                 out=n_grouped[unit][:].rearrange("p (c i j) -> p c j i", i=4, j=PACK),
-                in_=n_planes[:].rearrange("p (j c i) -> p c j i", j=PACK, i=4),
+                in_=n_planes[unit][:].rearrange("p (j c i) -> p c j i", j=PACK, i=4),
             )
 
         def quantise_features(unit):
-            n_mx[unit] = quantise(n_grouped[unit], CHUNK, "n_%d_%d" % unit)
+            side, first, nodes = unit
+            quantise(n_codes[side], n_scales[side], slice(first, first + nodes), n_grouped[unit][:])
 
-        def negate_n2(chunk):
-            negated = keep.tile([P, CHUNK * PACK], BF16, name="n_negated_%d" % chunk, align_bytes=64)
-            nc.vector.tensor_scalar_mul(negated[:], n_grouped[1, chunk][:], -1.0)
-            return negated
+        def negate(unit):
+            side, first, nodes = unit
+            n2_negated[unit] = keep.tile([P, nodes * PACK], BF16, name="n_negated_%d" % first, align_bytes=64)
+            nc.vector.tensor_scalar_mul(n2_negated[unit][:], n_grouped[unit][:], -1.0)
 
-        def block(row_chunk, col_chunk):
-            n1_row_codes, n1_row_scales = n_mx[0, row_chunk]
-            m2_row_codes, m2_row_scales = minus_n2_mx[row_chunk]
-            n1_col_codes, n1_col_scales = n_mx[0, col_chunk]
-            n2_col_codes, n2_col_scales = n_mx[1, col_chunk]
-            acc = psum.tile([P, TILES, CHUNK], F32, tag="bank")
-            for r in range(TILES):
-                rows = slice(r * P, (r + 1) * P)
+        def quantise_negated(unit):
+            side, first, nodes = unit
+            quantise(minus_codes, minus_scales, slice(first, first + nodes), n2_negated[unit][:])
+
+        x_of = {}
+
+        def sums(block):
+            row, rows, first, nodes = block
+            widths = [256, 128] if nodes == 384 else [nodes]
+            acc = psum.tile([P, rows, nodes], F32, tag="bank")
+            pieces = [(i, sum(widths[:j]), widths[j]) for i in range(rows) for j in range(len(widths))]
+            for i, start, width in pieces:
+                tile_cols = slice((row + i) * P, (row + i + 1) * P)
+                cols = slice(first + start, first + start + width)
                 nc.tensor.matmul_mx(
-                    out=acc[:, r, :],
-                    lhsT=n1_row_codes[:, rows].bitcast(FP8X4),
-                    lhsT_scale=n1_row_scales[:, rows],
-                    rhs=n2_col_codes[:].bitcast(FP8X4),
-                    rhs_scale=n2_col_scales[:],
+                    out=acc[:, i, start : start + width],
+                    lhsT=n_codes[0][:, tile_cols].bitcast(FP8X4),
+                    lhsT_scale=n_scales[0][:, tile_cols],
+                    rhs=n_codes[1][:, cols].bitcast(FP8X4),
+                    rhs_scale=n_scales[1][:, cols],
                     start=True,
                     stop=False,
                 )
                 nc.tensor.matmul_mx(
-                    out=acc[:, r, :],
-                    lhsT=m2_row_codes[:, rows].bitcast(FP8X4),
-                    lhsT_scale=m2_row_scales[:, rows],
-                    rhs=n1_col_codes[:].bitcast(FP8X4),
-                    rhs_scale=n1_col_scales[:],
+                    out=acc[:, i, start : start + width],
+                    lhsT=minus_codes[:, tile_cols].bitcast(FP8X4),
+                    lhsT_scale=minus_scales[:, tile_cols],
+                    rhs=n_codes[0][:, cols].bitcast(FP8X4),
+                    rhs_scale=n_scales[0][:, cols],
                     start=False,
                     stop=True,
                 )
-            result = keep.tile([P, TILES, CHUNK], F32, name="result_%d_%d" % (row_chunk, col_chunk))
-            nc.scalar.activation(out=result[:], in_=acc[:], func=TANH, scale=ALPHA)
-            nc.vector.tensor_scalar_max(result[:], result[:], 0.0)
+            x_of[block] = keep.tile([P, rows, nodes], F32, name="x_%d_%d" % (row, first))
+            nc.scalar.activation(out=x_of[block][:], in_=acc[:], func=TANH, scale=ALPHA)
+
+        def store(block):
+            row, rows, first, nodes = block
+            nc.vector.tensor_scalar_max(x_of[block][:], x_of[block][:], 0.0)
             nc.sync.dma_start(
-                out=out[
-                    row_chunk * CHUNK : (row_chunk + 1) * CHUNK, col_chunk * CHUNK : (col_chunk + 1) * CHUNK
-                ].rearrange("(r p) n -> p r n", p=P),
-                in_=result[:],
+                out=out[row * P : (row + rows) * P, first : first + nodes].rearrange("(r p) n -> p r n", p=P),
+                in_=x_of[block][:],
             )
-
-        blocks = []
-        for chunk in range(CHUNKS):
-            blocks.extend([(earlier, chunk) for earlier in range(chunk)])
-            blocks.extend([(chunk, col_chunk) for col_chunk in range(chunk + 1)])
-        issued = [0]
-
-        def one_block(step):
-            if issued[0] < len(blocks) and step >= 2 * max(blocks[issued[0]]) + 1 + BLOCKS_AFTER:
-                block(*blocks[issued[0]])
-                issued[0] = issued[0] + 1
 
         keep_busy(3)
         flip(units[0])
         keep_busy(2)
-        regroup_weight(1, 0, nc.vector.tensor_copy)
-        regroup_weight(1, 1, nc.scalar.copy)
-        for side in (1, 0):
-            nc.vector.tensor_scalar_mul(bias3[side][:], bias_raw[side][:], ALPHA)
+        flip(units[1])
+        copy_flipped(units[0])
+        regroup_weight(1, 0)
+        regroup_weight(1, 1, "A")
         quantise_emb(units[0])
         quantise_weight(1, 0)
-        flip(units[1])
+        scale_biases()
+        copy_flipped(units[1])
         quantise_weight(1, 1)
+        features(units[0])
+        flip(units[2])
+        regroup_weight(0, 0)
         quantise_emb(units[1])
-        regroup_weight(0, 0, nc.vector.tensor_copy)
-        regroup_weight(0, 1, nc.vector.tensor_copy)
+        regroup_weight(0, 1)
+        copy_flipped(units[2])
+        features(units[1])
+        flip(units[3])
+        flip(units[4])
         quantise_weight(0, 0)
+        quantise_emb(units[2])
         quantise_weight(0, 1)
-
-        prepared = 2
-        for step in range(len(units)):
-            unit = units[step]
-            side, chunk = unit
-            features(unit)
-            one_block(step)
-            if side == 0:
-                negated = negate_n2(chunk)
-            flipped_now = units[prepared : step + AHEAD + 1]
-            prepared = prepared + len(flipped_now)
-            for later in flipped_now:
-                flip(later)
-            one_block(step)
-            quantise_features(unit)
-            for later in flipped_now:
-                quantise_emb(later)
-            one_block(step)
-            if side == 0:
-                minus_n2_mx[chunk] = quantise(negated, CHUNK, "minus_n2_%d" % chunk)
-        for row_chunk, col_chunk in blocks[issued[0] :]:
-            block(row_chunk, col_chunk)
+        regroup_features(units[0])
+        copy_flipped(units[3])
+        copy_flipped(units[4])
+        features(units[2])
+        flip(units[5])
+        regroup_features(units[1])
+        quantise_emb(units[3])
+        copy_flipped(units[5], "V")
+        quantise_emb(units[4])
+        quantise_features(units[0])
+        flip(units[6])
+        quantise_emb(units[5])
+        regroup_features(units[2])
+        quantise_features(units[1])
+        negate(units[0])
+        copy_flipped(units[6])
+        features(units[3])
+        flip(units[7])
+        quantise_emb(units[6])
+        regroup_features(units[3])
+        quantise_features(units[2])
+        negate(units[1])
+        quantise_negated(units[0])
+        copy_flipped(units[7])
+        features(units[4])
+        features(units[5])
+        quantise_emb(units[7])
+        regroup_features(units[4])
+        quantise_features(units[3])
+        quantise_negated(units[1])
+        sums((0, 2, 0, 256))
+        features(units[6])
+        sums((0, 2, 256, 256))
+        regroup_features(units[5])
+        quantise_features(units[4])
+        store((0, 2, 0, 256))
+        negate(units[4])
+        sums((2, 1, 0, 512))
+        features(units[7])
+        regroup_features(units[6])
+        quantise_features(units[5])
+        store((0, 2, 256, 256))
+        quantise_negated(units[4])
+        sums((3, 1, 0, 512))
+        sums((0, 2, 512, 256))
+        store((2, 1, 0, 512))
+        quantise_features(units[6])
+        regroup_features(units[7])
+        sums((2, 2, 512, 256))
+        store((3, 1, 0, 512))
+        negate(units[6])
+        sums((4, 1, 0, 512))
+        store((0, 2, 512, 256))
+        quantise_features(units[7])
+        sums((5, 1, 0, 512))
+        store((2, 2, 512, 256))
+        sums((4, 2, 512, 256))
+        sums((0, 2, 768, 256))
+        store((4, 1, 0, 512))
+        quantise_negated(units[6])
+        sums((2, 2, 768, 256))
+        store((5, 1, 0, 512))
+        sums((4, 2, 768, 256))
+        store((4, 2, 512, 256))
+        sums((6, 1, 0, 512))
+        store((0, 2, 768, 256))
+        store((2, 2, 768, 256))
+        sums((6, 1, 512, 512))
+        store((4, 2, 768, 256))
+        sums((7, 1, 0, 512))
+        store((6, 1, 0, 512))
+        sums((7, 1, 512, 512))
+        store((6, 1, 512, 512))
+        store((7, 1, 0, 512))
+        store((7, 1, 512, 512))

@@ -262,8 +262,8 @@ def tile_gcn_pa_kernel(tc, emb1, emb2, lin1_w, lin1_b, lin2_w, lin2_b, out):
         flip(units[3])
         flip(units[4])
         quantise_weight(0, 0)
-        quantise_emb(units[2])
         quantise_weight(0, 1)
+        quantise_emb(units[2])
         regroup_features(units[0])
         copy_flipped(units[3])
         copy_flipped(units[4])
@@ -282,60 +282,62 @@ def tile_gcn_pa_kernel(tc, emb1, emb2, lin1_w, lin1_b, lin2_w, lin2_b, out):
         copy_flipped(units[6])
         features(units[3])
         flip(units[7])
-        quantise_emb(units[6])
-        regroup_features(units[3])
-        quantise_features(units[2])
-        negate(units[1])
-        quantise_negated(units[0])
-        copy_flipped(units[7])
         features(units[4])
+        keep_busy(3)
+        quantise_features(units[2])
+        quantise_negated(units[0])
+        regroup_features(units[3])
+        negate(units[1])
+        copy_flipped(units[7], "V")
+        sums((0, 2, 0, 256))
         features(units[5])
+        quantise_features(units[3])
+        store((0, 2, 0, 256))
+        quantise_negated(units[1])
+        quantise_emb(units[6])
         quantise_emb(units[7])
         regroup_features(units[4])
-        quantise_features(units[3])
-        quantise_negated(units[1])
-        sums((0, 2, 0, 256))
-        features(units[6])
         sums((0, 2, 256, 256))
-        regroup_features(units[5])
-        quantise_features(units[4])
-        store((0, 2, 0, 256))
-        negate(units[4])
         sums((2, 1, 0, 512))
-        features(units[7])
-        regroup_features(units[6])
-        quantise_features(units[5])
         store((0, 2, 256, 256))
-        quantise_negated(units[4])
+        quantise_features(units[4])
+        negate(units[4])
         sums((3, 1, 0, 512))
-        sums((0, 2, 512, 256))
+        features(units[6])
+        regroup_features(units[5])
+        quantise_negated(units[4])
+        quantise_features(units[5])
         store((2, 1, 0, 512))
-        quantise_features(units[6])
-        regroup_features(units[7])
-        sums((2, 2, 512, 256))
         store((3, 1, 0, 512))
-        negate(units[6])
-        sums((4, 1, 0, 512))
+        features(units[7])
+        keep_busy(3)
+        sums((0, 2, 512, 256))
+        regroup_features(units[6])
+        regroup_features(units[7])
         store((0, 2, 512, 256))
-        quantise_features(units[7])
-        sums((5, 1, 0, 512))
+        sums((2, 2, 512, 256))
+        quantise_features(units[6])
+        sums((4, 1, 0, 512))
         store((2, 2, 512, 256))
-        sums((4, 2, 512, 256))
-        sums((0, 2, 768, 256))
+        sums((5, 1, 0, 512))
         store((4, 1, 0, 512))
-        quantise_negated(units[6])
-        sums((2, 2, 768, 256))
+        quantise_features(units[7])
+        negate(units[6])
+        sums((4, 2, 512, 256))
         store((5, 1, 0, 512))
-        sums((4, 2, 768, 256))
+        quantise_negated(units[6])
+        sums((0, 2, 768, 256))
         store((4, 2, 512, 256))
-        sums((6, 1, 0, 512))
+        sums((2, 2, 768, 256))
         store((0, 2, 768, 256))
+        sums((4, 2, 768, 256))
         store((2, 2, 768, 256))
-        sums((6, 1, 512, 512))
+        sums((6, 1, 0, 512))
         store((4, 2, 768, 256))
-        sums((7, 1, 0, 512))
+        sums((6, 1, 512, 512))
         store((6, 1, 0, 512))
-        sums((7, 1, 512, 512))
+        sums((7, 1, 0, 512))
         store((6, 1, 512, 512))
+        sums((7, 1, 512, 512))
         store((7, 1, 0, 512))
         store((7, 1, 512, 512))

@@ -184,8 +184,8 @@ def tile_gcn_pa_kernel(tc, emb1, emb2, lin1_w, lin1_b, lin2_w, lin2_b, out):
             side, first, nodes = unit
             n_grouped[unit] = keep.tile([P, nodes * PACK], BF16, name="n_grouped_%d_%d" % (side, first), align_bytes=64)
             nc.vector.tensor_copy(
-                out=n_grouped[unit][:].rearrange("p (c i j) -> p c j i", i=4, j=PACK),
-                in_=n_planes[unit][:].rearrange("p (j c i) -> p c j i", j=PACK, i=4),
+                out=n_grouped[unit][:].rearrange("p (c i j) -> p c j i", i=8, j=PACK),
+                in_=n_planes[unit][:].rearrange("p (j c i) -> p c j i", j=PACK, i=8),
             )
 
         def quantise_features(unit):

@@ -202,6 +202,7 @@ def tile_gcn_pa_kernel(tc, emb1, emb2, lin1_w, lin1_b, lin2_w, lin2_b, out):
             quantise(minus_codes, minus_scales, slice(first, first + nodes), n2_negated[unit][:])
 
         x_of = {}
+        turned_of = {}
 
         def sums(block):
             row, rows, first, nodes = block
@@ -234,10 +235,43 @@ def tile_gcn_pa_kernel(tc, emb1, emb2, lin1_w, lin1_b, lin2_w, lin2_b, out):
 
         def store(block):
             row, rows, first, nodes = block
-            nc.vector.tensor_scalar_max(x_of[block][:], x_of[block][:], 0.0)
+            result = keep.tile([P, rows, nodes], F32, name="result_%d_%d" % (row, first))
+            nc.vector.tensor_scalar_max(result[:], x_of[block][:], 0.0)
             nc.sync.dma_start(
                 out=out[row * P : (row + rows) * P, first : first + nodes].rearrange("(r p) n -> p r n", p=P),
-                in_=x_of[block][:],
+                in_=result[:],
+            )
+
+        def turn(block):
+            row, rows, first, nodes = block
+            turned_of[block] = psum.tile([P, nodes // P, rows * P], F32, tag="bank", name="turned_%d_%d" % (row, first))
+            for c in range(nodes // P):
+                for r in range(rows):
+                    nc.tensor.transpose(
+                        turned_of[block][:, c, r * P : (r + 1) * P],
+                        x_of[block][:, r, c * P : (c + 1) * P],
+                        identity[:],
+                    )
+
+        def store_turned(block, engine="V"):
+            row, rows, first, nodes = block
+            mirrored = keep.tile([P, nodes // P, rows * P], F32, name="mirrored_%d_%d" % (row, first))
+            if engine == "A":
+                nc.scalar.activation(
+                    out=mirrored[:], in_=turned_of[block][:], func=mybir.ActivationFunctionType.Relu, scale=-1.0
+                )
+            else:
+                nc.vector.tensor_scalar(
+                    out=mirrored[:],
+                    in0=turned_of[block][:],
+                    scalar1=-1.0,
+                    scalar2=0.0,
+                    op0=mybir.AluOpType.mult,
+                    op1=mybir.AluOpType.max,
+                )
+            nc.sync.dma_start(
+                out=out[first : first + nodes, row * P : (row + rows) * P].rearrange("(r p) n -> p r n", p=P),
+                in_=mirrored[:],
             )
 
         keep_busy(3)
@@ -298,17 +332,17 @@ def tile_gcn_pa_kernel(tc, emb1, emb2, lin1_w, lin1_b, lin2_w, lin2_b, out):
         quantise_emb(units[7])
         regroup_features(units[4])
         sums((0, 2, 256, 256))
-        sums((2, 1, 0, 512))
+        sums((2, 2, 256, 256))
         store((0, 2, 256, 256))
         quantise_features(units[4])
         negate(units[4])
-        sums((3, 1, 0, 512))
         features(units[6])
+        turn((0, 2, 256, 256))
         regroup_features(units[5])
         quantise_negated(units[4])
         quantise_features(units[5])
-        store((2, 1, 0, 512))
-        store((3, 1, 0, 512))
+        store((2, 2, 256, 256))
+        store_turned((0, 2, 256, 256), "A")
         features(units[7])
         keep_busy(3)
         sums((0, 2, 512, 256))
@@ -317,27 +351,27 @@ def tile_gcn_pa_kernel(tc, emb1, emb2, lin1_w, lin1_b, lin2_w, lin2_b, out):
         store((0, 2, 512, 256))
         sums((2, 2, 512, 256))
         quantise_features(units[6])
-        sums((4, 1, 0, 512))
+        sums((4, 2, 512, 256))
+        turn((0, 2, 512, 256))
         store((2, 2, 512, 256))
-        sums((5, 1, 0, 512))
-        store((4, 1, 0, 512))
+        store_turned((0, 2, 512, 256), "A")
+        turn((2, 2, 512, 256))
         quantise_features(units[7])
         negate(units[6])
-        sums((4, 2, 512, 256))
-        store((5, 1, 0, 512))
+        store_turned((2, 2, 512, 256), "A")
+        store((4, 2, 512, 256))
         quantise_negated(units[6])
         sums((0, 2, 768, 256))
-        store((4, 2, 512, 256))
         sums((2, 2, 768, 256))
         store((0, 2, 768, 256))
         sums((4, 2, 768, 256))
+        turn((0, 2, 768, 256))
         store((2, 2, 768, 256))
-        sums((6, 1, 0, 512))
+        sums((6, 2, 768, 256))
+        turn((2, 2, 768, 256))
+        store_turned((0, 2, 768, 256))
         store((4, 2, 768, 256))
-        sums((6, 1, 512, 512))
-        store((6, 1, 0, 512))
-        sums((7, 1, 0, 512))
-        store((6, 1, 512, 512))
-        sums((7, 1, 512, 512))
-        store((7, 1, 0, 512))
-        store((7, 1, 512, 512))
+        turn((4, 2, 768, 256))
+        store_turned((2, 2, 768, 256), "A")
+        store((6, 2, 768, 256))
+        store_turned((4, 2, 768, 256))

@@ -56,10 +56,9 @@ def tile_gcn_pa_kernel(tc, emb1, emb2, lin1_w, lin1_b, lin2_w, lin2_b, out):
         for unit in units[2:]:
             load_unit(unit)
 
-        bias_raw = {}
+        bias_raw = keep.tile([P, 2, 16], BF16, name="bias_raw")
         for side in (1, 0):
-            bias_raw[side] = keep.tile([P, PACK], BF16, name="bias_raw_%d" % side)
-            nc.scalar.dma_start(out=bias_raw[side][:], in_=biases[side].rearrange("(p j) -> p j", j=PACK))
+            nc.scalar.dma_start(out=bias_raw[:, side, :PACK], in_=biases[side].rearrange("(p j) -> p j", j=PACK))
 
         identity = keep.tile([P, P], F32, name="identity")
         make_identity(nc, identity[:])
@@ -80,14 +79,13 @@ def tile_gcn_pa_kernel(tc, emb1, emb2, lin1_w, lin1_b, lin2_w, lin2_b, out):
         w_grouped = {}
         w_codes = {}
         w_scales = {}
-        bias3 = {}
+        bias3 = keep.tile([P, 2, PACK], F32, name="bias3")
         n_codes = {}
         n_scales = {}
         for side in (1, 0):
             w_grouped[side] = keep.tile([P, DIM * PACK], BF16, name="w_grouped_%d" % side, align_bytes=64)
             w_codes[side] = keep.tile([P, DIM], U32, name="codes_w_%d" % side, align_bytes=64)
             w_scales[side] = keep.tile([P, DIM], U8, name="scales_w_%d" % side, align_bytes=64)
-            bias3[side] = keep.tile([P, PACK], F32, name="bias3_%d" % side)
             n_codes[side] = keep.tile([P, NODES], U32, name="codes_n_%d" % side, align_bytes=64)
             n_scales[side] = keep.tile([P, NODES], U8, name="scales_n_%d" % side, align_bytes=64)
         minus_codes = keep.tile([P, NODES], U32, name="codes_minus", align_bytes=64)
@@ -102,16 +100,15 @@ def tile_gcn_pa_kernel(tc, emb1, emb2, lin1_w, lin1_b, lin2_w, lin2_b, out):
             )
 
         def scale_biases():
-            for side in (1, 0):
-                nc.vector.tensor_scalar_mul(bias3[side][:], bias_raw[side][:], ALPHA)
+            nc.vector.tensor_scalar_mul(bias3[:], bias_raw[:, :, :PACK], ALPHA)
 
-        def quantise_weight(side, half):
-            cols = slice(half * DIM // 2, (half + 1) * DIM // 2)
+        def quantise_weight(side, half, halves=1):
+            cols = slice(half * DIM // 2, (half + halves) * DIM // 2)
             quantise(
                 w_codes[side],
                 w_scales[side],
                 cols,
-                w_grouped[side][:, half * DIM * PACK // 2 : (half + 1) * DIM * PACK // 2],
+                w_grouped[side][:, half * DIM * PACK // 2 : (half + halves) * DIM * PACK // 2],
             )
 
         emb_grouped = {}
@@ -176,7 +173,7 @@ def tile_gcn_pa_kernel(tc, emb1, emb2, lin1_w, lin1_b, lin2_w, lin2_b, out):
                         out=n_planes[unit][:, j * nodes : (j + 1) * nodes],
                         in_=acc[:, i, :],
                         func=TANH,
-                        bias=bias3[side][:, j : j + 1],
+                        bias=bias3[:, side, j : j + 1],
                         scale=ALPHA,
                     )
 
@@ -203,17 +200,23 @@ def tile_gcn_pa_kernel(tc, emb1, emb2, lin1_w, lin1_b, lin2_w, lin2_b, out):
 
         x_of = {}
         turned_of = {}
+        above_of = {}
+        below_of = {}
 
-        def sums(block):
-            row, rows, first, nodes = block
-            widths = [256, 128] if nodes == 384 else [nodes]
+        def open_strip(strip):
+            first, nodes = strip
+            x_of[strip] = keep.tile([P, (first + nodes) // P, nodes], F32, name="x_%d" % first)
+            above_of[strip] = keep.tile([P, max(1, first // P), nodes], F32, name="above_%d" % first)
+            below_of[strip] = keep.tile([P, nodes // P, first + nodes], F32, name="below_%d" % first)
+
+        def sums(strip, row, rows):
+            first, nodes = strip
+            cols = slice(first, first + nodes)
             acc = psum.tile([P, rows, nodes], F32, tag="bank")
-            pieces = [(i, sum(widths[:j]), widths[j]) for i in range(rows) for j in range(len(widths))]
-            for i, start, width in pieces:
+            for i in range(rows):
                 tile_cols = slice((row + i) * P, (row + i + 1) * P)
-                cols = slice(first + start, first + start + width)
                 nc.tensor.matmul_mx(
-                    out=acc[:, i, start : start + width],
+                    out=acc[:, i, :],
                     lhsT=n_codes[0][:, tile_cols].bitcast(FP8X4),
                     lhsT_scale=n_scales[0][:, tile_cols],
                     rhs=n_codes[1][:, cols].bitcast(FP8X4),
@@ -222,7 +225,7 @@ def tile_gcn_pa_kernel(tc, emb1, emb2, lin1_w, lin1_b, lin2_w, lin2_b, out):
                     stop=False,
                 )
                 nc.tensor.matmul_mx(
-                    out=acc[:, i, start : start + width],
+                    out=acc[:, i, :],
                     lhsT=minus_codes[:, tile_cols].bitcast(FP8X4),
                     lhsT_scale=minus_scales[:, tile_cols],
                     rhs=n_codes[0][:, cols].bitcast(FP8X4),
@@ -230,50 +233,63 @@ def tile_gcn_pa_kernel(tc, emb1, emb2, lin1_w, lin1_b, lin2_w, lin2_b, out):
                     start=False,
                     stop=True,
                 )
-            x_of[block] = keep.tile([P, rows, nodes], F32, name="x_%d_%d" % (row, first))
-            nc.scalar.activation(out=x_of[block][:], in_=acc[:], func=TANH, scale=ALPHA)
+            nc.scalar.activation(out=x_of[strip][:, row : row + rows, :], in_=acc[:], func=TANH, scale=ALPHA)
 
-        def store(block):
-            row, rows, first, nodes = block
-            result = keep.tile([P, rows, nodes], F32, name="result_%d_%d" % (row, first))
-            nc.vector.tensor_scalar_max(result[:], x_of[block][:], 0.0)
-            nc.sync.dma_start(
-                out=out[row * P : (row + rows) * P, first : first + nodes].rearrange("(r p) n -> p r n", p=P),
-                in_=result[:],
-            )
-
-        def turn(block):
-            row, rows, first, nodes = block
-            turned_of[block] = psum.tile([P, nodes // P, rows * P], F32, tag="bank", name="turned_%d_%d" % (row, first))
+        def turn(strip, row, rows):
+            first, nodes = strip
+            turned = psum.tile([P, nodes // P, rows * P], F32, tag="bank")
             for c in range(nodes // P):
                 for r in range(rows):
                     nc.tensor.transpose(
-                        turned_of[block][:, c, r * P : (r + 1) * P],
-                        x_of[block][:, r, c * P : (c + 1) * P],
+                        turned[:, c, r * P : (r + 1) * P],
+                        x_of[strip][:, row + r, c * P : (c + 1) * P],
                         identity[:],
                     )
+            turned_of[strip, row] = turned
 
-        def store_turned(block, engine="V"):
-            row, rows, first, nodes = block
-            mirrored = keep.tile([P, nodes // P, rows * P], F32, name="mirrored_%d_%d" % (row, first))
+        def relu_above(strip, row, rows):
+            nc.vector.tensor_scalar_max(
+                above_of[strip][:, row : row + rows, :], x_of[strip][:, row : row + rows, :], 0.0
+            )
+
+        def relu_diagonal(strip):
+            first, nodes = strip
+            nc.vector.tensor_scalar_max(below_of[strip][:, :, first:], x_of[strip][:, first // P :, :], 0.0)
+
+        def relu_below(strip, row, rows, engine="V"):
+            result = below_of[strip][:, :, row * P : (row + rows) * P]
             if engine == "A":
                 nc.scalar.activation(
-                    out=mirrored[:], in_=turned_of[block][:], func=mybir.ActivationFunctionType.Relu, scale=-1.0
+                    out=result, in_=turned_of[strip, row][:], func=mybir.ActivationFunctionType.Relu, scale=-1.0
                 )
             else:
                 nc.vector.tensor_scalar(
-                    out=mirrored[:],
-                    in0=turned_of[block][:],
+                    out=result,
+                    in0=turned_of[strip, row][:],
                     scalar1=-1.0,
                     scalar2=0.0,
                     op0=mybir.AluOpType.mult,
                     op1=mybir.AluOpType.max,
                 )
+
+        def store_above(strip, row, rows):
+            first, nodes = strip
             nc.sync.dma_start(
-                out=out[first : first + nodes, row * P : (row + rows) * P].rearrange("(r p) n -> p r n", p=P),
-                in_=mirrored[:],
+                out=out[row * P : (row + rows) * P, first : first + nodes].rearrange("(r p) n -> p r n", p=P),
+                in_=above_of[strip][:, row : row + rows, :],
             )
 
+        def store_below(strip, col, cols):
+            first, nodes = strip
+            nc.sync.dma_start(
+                out=out[first : first + nodes, col * P : (col + cols) * P].rearrange("(r p) n -> p r n", p=P),
+                in_=below_of[strip][:, :, col * P : (col + cols) * P],
+            )
+
+        open_strip((0, 256))
+        open_strip((256, 256))
+        open_strip((512, 256))
+        open_strip((768, 256))
         keep_busy(3)
         flip(units[0])
         keep_busy(2)
@@ -303,75 +319,87 @@ def tile_gcn_pa_kernel(tc, emb1, emb2, lin1_w, lin1_b, lin2_w, lin2_b, out):
         copy_flipped(units[4])
         features(units[2])
         flip(units[5])
+        flip(units[6])
         regroup_features(units[1])
         quantise_emb(units[3])
         copy_flipped(units[5], "V")
         quantise_emb(units[4])
         quantise_features(units[0])
-        flip(units[6])
         quantise_emb(units[5])
         regroup_features(units[2])
-        quantise_features(units[1])
         negate(units[0])
         copy_flipped(units[6])
         features(units[3])
         flip(units[7])
         features(units[4])
-        keep_busy(3)
+        keep_busy(2)
         quantise_features(units[2])
         quantise_negated(units[0])
         regroup_features(units[3])
+        quantise_features(units[1])
         negate(units[1])
-        copy_flipped(units[7], "V")
-        sums((0, 2, 0, 256))
+        sums((0, 256), 0, 2)
         features(units[5])
         quantise_features(units[3])
-        store((0, 2, 0, 256))
+        copy_flipped(units[7], "V")
         quantise_negated(units[1])
+        relu_diagonal((0, 256))
+        store_below((0, 256), 0, 2)
         quantise_emb(units[6])
         quantise_emb(units[7])
         regroup_features(units[4])
-        sums((0, 2, 256, 256))
-        sums((2, 2, 256, 256))
-        store((0, 2, 256, 256))
-        quantise_features(units[4])
+        sums((256, 256), 0, 2)
+        sums((256, 256), 2, 2)
+        relu_above((256, 256), 0, 2)
+        store_above((256, 256), 0, 2)
         negate(units[4])
         features(units[6])
-        turn((0, 2, 256, 256))
+        turn((256, 256), 0, 2)
         regroup_features(units[5])
-        quantise_negated(units[4])
+        quantise_features(units[4])
         quantise_features(units[5])
-        store((2, 2, 256, 256))
-        store_turned((0, 2, 256, 256), "A")
+        quantise_negated(units[4])
+        relu_diagonal((256, 256))
+        relu_below((256, 256), 0, 2, "A")
+        store_below((256, 256), 0, 4)
         features(units[7])
-        keep_busy(3)
-        sums((0, 2, 512, 256))
+        keep_busy(2)
+        sums((512, 256), 0, 2)
         regroup_features(units[6])
         regroup_features(units[7])
-        store((0, 2, 512, 256))
-        sums((2, 2, 512, 256))
+        relu_above((512, 256), 0, 2)
+        store_above((512, 256), 0, 2)
+        sums((512, 256), 2, 2)
         quantise_features(units[6])
-        sums((4, 2, 512, 256))
-        turn((0, 2, 512, 256))
-        store((2, 2, 512, 256))
-        store_turned((0, 2, 512, 256), "A")
-        turn((2, 2, 512, 256))
+        turn((512, 256), 0, 2)
+        relu_above((512, 256), 2, 2)
+        store_above((512, 256), 2, 2)
+        relu_below((512, 256), 0, 2, "A")
+        turn((512, 256), 2, 2)
         quantise_features(units[7])
         negate(units[6])
-        store_turned((2, 2, 512, 256), "A")
-        store((4, 2, 512, 256))
+        relu_below((512, 256), 2, 2, "A")
+        sums((512, 256), 4, 2)
+        store_below((512, 256), 0, 4)
+        relu_diagonal((512, 256))
+        store_below((512, 256), 4, 2)
         quantise_negated(units[6])
-        sums((0, 2, 768, 256))
-        sums((2, 2, 768, 256))
-        store((0, 2, 768, 256))
-        sums((4, 2, 768, 256))
-        turn((0, 2, 768, 256))
-        store((2, 2, 768, 256))
-        sums((6, 2, 768, 256))
-        turn((2, 2, 768, 256))
-        store_turned((0, 2, 768, 256))
-        store((4, 2, 768, 256))
-        turn((4, 2, 768, 256))
-        store_turned((2, 2, 768, 256), "A")
-        store((6, 2, 768, 256))
-        store_turned((4, 2, 768, 256))
+        sums((768, 256), 0, 2)
+        sums((768, 256), 2, 2)
+        relu_above((768, 256), 0, 2)
+        store_above((768, 256), 0, 2)
+        sums((768, 256), 4, 2)
+        turn((768, 256), 0, 2)
+        relu_above((768, 256), 2, 2)
+        store_above((768, 256), 2, 2)
+        sums((768, 256), 6, 2)
+        turn((768, 256), 2, 2)
+        relu_below((768, 256), 0, 2)
+        relu_above((768, 256), 4, 2)
+        store_above((768, 256), 4, 2)
+        turn((768, 256), 4, 2)
+        relu_below((768, 256), 2, 2)
+        store_below((768, 256), 0, 4)
+        relu_diagonal((768, 256))
+        relu_below((768, 256), 4, 2)
+        store_below((768, 256), 4, 4)

import concourse.mybir as mybir
from concourse.masks import make_identity

FP8X4 = mybir.dt.float8_e4m3fn_x4
BF16 = mybir.dt.bfloat16
F32 = mybir.dt.float32
U32 = mybir.dt.uint32
U8 = mybir.dt.uint8
TANH = mybir.ActivationFunctionType.Tanh

P = 128
PACK = 4
NODES = 1024
DIM = 512
ALPHA = 3.0
BANK = 512
WORDS = DIM // 2

FLOPS = 2 * (2 * NODES * DIM * DIM) + 2 * (2 * NODES * NODES * DIM)


def tile_gcn_pa_kernel(tc, emb1, emb2, lin1_w, lin1_b, lin2_w, lin2_b, out):
    nc = tc.nc
    embs = (emb1, emb2)
    weights = (lin1_w, lin2_w)
    biases = (lin1_b, lin2_b)
    units = [(1, 0, 256), (1, 256, 256), (0, 0, 256), (0, 256, 256), (1, 512, 256), (0, 512, 256), (1, 768, 256), (0, 768, 256)]

    with tc.tile_pool(name="keep", bufs=1) as keep, tc.psum_pool(name="psum", bufs=8) as psum, tc.manual_schedule():

        def quantise(codes, scales, cols, grouped):
            nc.vector.quantize_mx(out=codes[:, cols].bitcast(FP8X4), scales=scales[:, cols], in_=grouped)

        w_raw = {}
        emb_raw = {}

        def load_weight(side):
            w_raw[side] = keep.tile([P, PACK * DIM], BF16, name="w_raw_%d" % side)
            nc.sync.dma_start(
                out=w_raw[side][:].rearrange("p (u ec) -> p u ec", u=2),
                in_=weights[side].rearrange("(u p e) c -> p u (e c)", u=2, e=2),
            )

        def load_unit(unit):
            side, first, nodes = unit
            emb_raw[unit] = keep.tile([P, nodes // P * DIM], BF16, name="emb_raw_%d_%d" % (side, first))
            nc.sync.dma_start(
                out=emb_raw[unit][:].rearrange("p (r k) -> p r k", k=DIM),
                in_=embs[side][first : first + nodes, :].rearrange("(r p) k -> p r k", p=P),
            )

        load_unit(units[0])
        load_weight(1)
        load_unit(units[1])
        load_weight(0)
        for unit in units[2:]:
            load_unit(unit)

        bias_raw = keep.tile([P, 2, 16], BF16, name="bias_raw")
        for side in (1, 0):
            nc.scalar.dma_start(out=bias_raw[:, side, :PACK], in_=biases[side].rearrange("(p j) -> p j", j=PACK))

        identity = keep.tile([P, P], F32, name="identity")
        make_identity(nc, identity[:])

        zero = keep.tile([P, 1], F32, name="zero")
        warm = keep.tile([P, 1], F32, name="warm")
        nc.vector.memset(zero[:], 0.0)
        nc.scalar.activation(out=warm[:], in_=zero[:], func=TANH)

        idle = keep.tile([P, BANK], BF16, name="idle")
        nc.vector.memset(idle[:], 0.0)

        def keep_busy(times):
            for i in range(times):
                unread = psum.tile([P, BANK], F32, tag="bank")
                nc.tensor.matmul(unread[:], lhsT=idle[:, :P], rhs=idle[:], start=True, stop=True)

        w_grouped = {}
        w_codes = {}
        w_scales = {}
        bias3 = keep.tile([P, 2, PACK], F32, name="bias3")
        n_codes = {}
        n_scales = {}
        for side in (1, 0):
            w_grouped[side] = keep.tile([P, DIM * PACK], BF16, name="w_grouped_%d" % side, align_bytes=64)
            w_codes[side] = keep.tile([P, DIM], U32, name="codes_w_%d" % side, align_bytes=64)
            w_scales[side] = keep.tile([P, DIM], U8, name="scales_w_%d" % side, align_bytes=64)
            n_codes[side] = keep.tile([P, NODES], U32, name="codes_n_%d" % side, align_bytes=64)
            n_scales[side] = keep.tile([P, NODES], U8, name="scales_n_%d" % side, align_bytes=64)
        minus_codes = keep.tile([P, NODES], U32, name="codes_minus", align_bytes=64)
        minus_scales = keep.tile([P, NODES], U8, name="scales_minus", align_bytes=64)

        def regroup_weight(side, half, engine="V"):
            tiles = slice(2 * half, 2 * half + 2)
            copy = nc.scalar.copy if engine == "A" else nc.vector.tensor_copy
            copy(
                out=w_grouped[side][:].rearrange("p (j q t) -> p q t j", j=PACK, t=PACK)[:, :, :, tiles],
                in_=w_raw[side][:].rearrange("p (t q j) -> p q t j", t=PACK, j=PACK)[:, :, :, tiles],
            )

        def scale_biases():
            nc.vector.tensor_scalar_mul(bias3[:], bias_raw[:, :, :PACK], ALPHA)

        def quantise_weight(side, half, halves=1):
            cols = slice(half * DIM // 2, (half + halves) * DIM // 2)
            quantise(
                w_codes[side],
                w_scales[side],
                cols,
                w_grouped[side][:, half * DIM * PACK // 2 : (half + halves) * DIM * PACK // 2],
            )

        emb_grouped = {}
        emb_codes = {}
        emb_scales = {}

        flipped_of = {}

        def flip(unit):
            side, first, nodes = unit
            words = emb_raw[unit][:].bitcast(F32)
            flipped_of[unit] = psum.tile([P, 2, nodes], F32, tag="bank", name="flipped_%d_%d" % (side, first))
            for r in range(nodes // P):
                for u in range(2):
                    nc.tensor.transpose(
                        flipped_of[unit][:, u, r * P : (r + 1) * P],
                        words[:, r * WORDS + u * P : r * WORDS + (u + 1) * P],
                        identity[:],
                    )

        def copy_flipped(unit, engine="A"):
            side, first, nodes = unit
            emb_grouped[unit] = keep.tile(
                [P, nodes * PACK], BF16, name="emb_grouped_%d_%d" % (side, first), align_bytes=64
            )
            copy = nc.scalar.copy if engine == "A" else nc.vector.tensor_copy
            copy(
                out=emb_grouped[unit][:].bitcast(F32).rearrange("p (n u) -> p n u", u=2),
                in_=flipped_of[unit][:].rearrange("p u n -> p n u"),
            )

        def quantise_emb(unit):
            side, first, nodes = unit
            emb_codes[unit] = keep.tile([P, nodes], U32, name="codes_emb_%d_%d" % (side, first), align_bytes=64)
            emb_scales[unit] = keep.tile([P, nodes], U8, name="scales_emb_%d_%d" % (side, first), align_bytes=64)
            quantise(emb_codes[unit], emb_scales[unit], slice(0, nodes), emb_grouped[unit][:])

        n_planes = {}
        n_grouped = {}
        n2_negated = {}

        def features(unit):
            side, first, nodes = unit
            n_planes[unit] = keep.tile([P, PACK * nodes], BF16, name="n_planes_%d_%d" % (side, first))
            per_bank = BANK // nodes
            for j0 in range(0, PACK, per_bank):
                acc = psum.tile([P, per_bank, nodes], F32, tag="bank")
                for i in range(per_bank):
                    cols = slice((j0 + i) * P, (j0 + i + 1) * P)
                    nc.tensor.matmul_mx(
                        out=acc[:, i, :],
                        lhsT=w_codes[side][:, cols].bitcast(FP8X4),
                        lhsT_scale=w_scales[side][:, cols],
                        rhs=emb_codes[unit][:].bitcast(FP8X4),
                        rhs_scale=emb_scales[unit][:],
                        start=True,
                        stop=True,
                    )
                for i in range(per_bank):
                    j = j0 + i
                    nc.scalar.activation(
                        out=n_planes[unit][:, j * nodes : (j + 1) * nodes],
                        in_=acc[:, i, :],
                        func=TANH,
                        bias=bias3[:, side, j : j + 1],
                        scale=ALPHA,
                    )

        def regroup_features(unit):
            side, first, nodes = unit
            n_grouped[unit] = keep.tile([P, nodes * PACK], BF16, name="n_grouped_%d_%d" % (side, first), align_bytes=64)
            nc.vector.tensor_copy(
                out=n_grouped[unit][:].rearrange("p (c i j) -> p c j i", i=8, j=PACK),
                in_=n_planes[unit][:].rearrange("p (j c i) -> p c j i", j=PACK, i=8),
            )

        def quantise_features(unit):
            side, first, nodes = unit
            quantise(n_codes[side], n_scales[side], slice(first, first + nodes), n_grouped[unit][:])

        def negate(unit):
            side, first, nodes = unit
            n2_negated[unit] = keep.tile([P, nodes * PACK], BF16, name="n_negated_%d" % first, align_bytes=64)
            nc.vector.tensor_scalar_mul(n2_negated[unit][:], n_grouped[unit][:], -1.0)

        def quantise_negated(unit):
            side, first, nodes = unit
            quantise(minus_codes, minus_scales, slice(first, first + nodes), n2_negated[unit][:])

        x_of = {}
        turned_of = {}
        above_of = {}
        below_of = {}

        def open_strip(strip):
            first, nodes = strip
            x_of[strip] = keep.tile([P, (first + nodes) // P, nodes], F32, name="x_%d" % first)
            above_of[strip] = keep.tile([P, max(1, first // P), nodes], F32, name="above_%d" % first)
            below_of[strip] = keep.tile([P, nodes // P, first + nodes], F32, name="below_%d" % first)

        def sums(strip, row, rows):
            first, nodes = strip
            cols = slice(first, first + nodes)
            acc = psum.tile([P, rows, nodes], F32, tag="bank")
            for i in range(rows):
                tile_cols = slice((row + i) * P, (row + i + 1) * P)
                nc.tensor.matmul_mx(
                    out=acc[:, i, :],
                    lhsT=n_codes[0][:, tile_cols].bitcast(FP8X4),
                    lhsT_scale=n_scales[0][:, tile_cols],
                    rhs=n_codes[1][:, cols].bitcast(FP8X4),
                    rhs_scale=n_scales[1][:, cols],
                    start=True,
                    stop=False,
                )
                nc.tensor.matmul_mx(
                    out=acc[:, i, :],
                    lhsT=minus_codes[:, tile_cols].bitcast(FP8X4),
                    lhsT_scale=minus_scales[:, tile_cols],
                    rhs=n_codes[0][:, cols].bitcast(FP8X4),
                    rhs_scale=n_scales[0][:, cols],
                    start=False,
                    stop=True,
                )
            nc.scalar.activation(out=x_of[strip][:, row : row + rows, :], in_=acc[:], func=TANH, scale=ALPHA)

        def turn(strip, row, rows):
            first, nodes = strip
            turned = psum.tile([P, nodes // P, rows * P], F32, tag="bank")
            for c in range(nodes // P):
                for r in range(rows):
                    nc.tensor.transpose(
                        turned[:, c, r * P : (r + 1) * P],
                        x_of[strip][:, row + r, c * P : (c + 1) * P],
                        identity[:],
                    )
            turned_of[strip, row] = turned

        def relu_above(strip, row, rows):
            nc.vector.tensor_scalar_max(
                above_of[strip][:, row : row + rows, :], x_of[strip][:, row : row + rows, :], 0.0
            )

        def relu_diagonal(strip):
            first, nodes = strip
            nc.vector.tensor_scalar_max(below_of[strip][:, :, first:], x_of[strip][:, first // P :, :], 0.0)

        def relu_below(strip, row, rows, engine="V"):
            result = below_of[strip][:, :, row * P : (row + rows) * P]
            if engine == "A":
                nc.scalar.activation(
                    out=result, in_=turned_of[strip, row][:], func=mybir.ActivationFunctionType.Relu, scale=-1.0
                )
            else:
                nc.vector.tensor_scalar(
                    out=result,
                    in0=turned_of[strip, row][:],
                    scalar1=-1.0,
                    scalar2=0.0,
                    op0=mybir.AluOpType.mult,
                    op1=mybir.AluOpType.max,
                )

        def store_above(strip, row, rows):
            first, nodes = strip
            nc.sync.dma_start(
                out=out[row * P : (row + rows) * P, first : first + nodes].rearrange("(r p) n -> p r n", p=P),
                in_=above_of[strip][:, row : row + rows, :],
            )

        def store_below(strip, col, cols):
            first, nodes = strip
            nc.sync.dma_start(
                out=out[first : first + nodes, col * P : (col + cols) * P].rearrange("(r p) n -> p r n", p=P),
                in_=below_of[strip][:, :, col * P : (col + cols) * P],
            )

        open_strip((0, 256))
        open_strip((256, 256))
        open_strip((512, 256))
        open_strip((768, 256))
        keep_busy(3)
        flip(units[0])
        keep_busy(2)
        flip(units[1])
        copy_flipped(units[0])
        regroup_weight(1, 0)
        regroup_weight(1, 1, "A")
        quantise_emb(units[0])
        quantise_weight(1, 0)
        scale_biases()
        copy_flipped(units[1])
        quantise_weight(1, 1)
        features(units[0])
        flip(units[2])
        regroup_weight(0, 0)
        quantise_emb(units[1])
        regroup_weight(0, 1)
        copy_flipped(units[2])
        features(units[1])
        flip(units[3])
        flip(units[4])
        quantise_weight(0, 0)
        quantise_weight(0, 1)
        quantise_emb(units[2])
        regroup_features(units[0])
        copy_flipped(units[3])
        copy_flipped(units[4])
        features(units[2])
        flip(units[5])
        flip(units[6])
        regroup_features(units[1])
        quantise_emb(units[3])
        copy_flipped(units[5], "V")
        quantise_emb(units[4])
        quantise_features(units[0])
        quantise_emb(units[5])
        regroup_features(units[2])
        negate(units[0])
        copy_flipped(units[6])
        features(units[3])
        flip(units[7])
        features(units[4])
        keep_busy(2)
        quantise_features(units[2])
        quantise_negated(units[0])
        regroup_features(units[3])
        quantise_features(units[1])
        negate(units[1])
        sums((0, 256), 0, 2)
        features(units[5])
        quantise_features(units[3])
        copy_flipped(units[7], "V")
        quantise_negated(units[1])
        relu_diagonal((0, 256))
        store_below((0, 256), 0, 2)
        quantise_emb(units[6])
        quantise_emb(units[7])
        regroup_features(units[4])
        sums((256, 256), 0, 2)
        sums((256, 256), 2, 2)
        relu_above((256, 256), 0, 2)
        store_above((256, 256), 0, 2)
        negate(units[4])
        features(units[6])
        turn((256, 256), 0, 2)
        regroup_features(units[5])
        quantise_features(units[4])
        quantise_features(units[5])
        quantise_negated(units[4])
        relu_diagonal((256, 256))
        relu_below((256, 256), 0, 2, "A")
        store_below((256, 256), 0, 4)
        features(units[7])
        keep_busy(2)
        sums((512, 256), 0, 2)
        regroup_features(units[6])
        regroup_features(units[7])
        relu_above((512, 256), 0, 2)
        store_above((512, 256), 0, 2)
        sums((512, 256), 2, 2)
        quantise_features(units[6])
        turn((512, 256), 0, 2)
        relu_above((512, 256), 2, 2)
        store_above((512, 256), 2, 2)
        relu_below((512, 256), 0, 2, "A")
        turn((512, 256), 2, 2)
        quantise_features(units[7])
        negate(units[6])
        relu_below((512, 256), 2, 2, "A")
        sums((512, 256), 4, 2)
        store_below((512, 256), 0, 4)
        relu_diagonal((512, 256))
        store_below((512, 256), 4, 2)
        quantise_negated(units[6])
        sums((768, 256), 0, 2)
        sums((768, 256), 2, 2)
        relu_above((768, 256), 0, 2)
        store_above((768, 256), 0, 2)
        sums((768, 256), 4, 2)
        turn((768, 256), 0, 2)
        relu_above((768, 256), 2, 2)
        store_above((768, 256), 2, 2)
        sums((768, 256), 6, 2)
        turn((768, 256), 2, 2)
        relu_below((768, 256), 0, 2)
        relu_above((768, 256), 4, 2)
        store_above((768, 256), 4, 2)
        turn((768, 256), 4, 2)
        relu_below((768, 256), 2, 2)
        store_below((768, 256), 0, 4)
        relu_diagonal((768, 256))
        relu_below((768, 256), 4, 2)
        store_below((768, 256), 4, 4)
